import numpy as np
import ml_dtypes


def mxq(x, axis, fmt="e4m3"):
    dtype, down = {"e4m3": (ml_dtypes.float8_e4m3fn, 7), "e5m2": (ml_dtypes.float8_e5m2, 14)}[fmt]
    v = np.moveaxis(np.asarray(x, np.float32).astype(ml_dtypes.bfloat16).astype(np.float64), axis, -1)
    blocks = v.reshape(v.shape[:-1] + (-1, 32))
    amax = np.abs(blocks).max(-1, keepdims=True)
    byte = np.maximum(np.where(amax > 0, np.frexp(amax)[1] - 1 + 127, 0) - down, 1)
    scale = np.exp2(byte - 127.0)
    codes = (blocks / scale).astype(np.float32).astype(dtype).astype(np.float64)
    return np.moveaxis((codes * scale).reshape(v.shape), -1, axis)


WIDE = False


def mx_kscale(k):
    if not WIDE:
        return np.ones(k)
    levels = np.array([10, -10, 5, -5, 0])
    a = np.random.permutation(np.resize(levels, k // 512 * 4)).reshape(k // 512, 4)
    idx = np.arange(k)
    return np.exp2(a[idx // 512, idx % 128 // 32])


BF16 = ml_dtypes.bfloat16


def bf(x):
    return np.asarray(x, np.float32).astype(BF16)


def f64(x):
    return np.asarray(x).astype(np.float64)


E2M1 = np.array([0.0, 0.5, 1.0, 1.5, 2.0, 3.0, 4.0, 6.0, -0.0, -0.5, -1.0, -1.5, -2.0, -3.0, -4.0, -6.0])


def pack_weight(w, fmt):
    k, n = w.shape
    w = f64(bf(w)).reshape(k // 32, 32, n)
    amax = np.abs(w).max(1)
    if fmt == "e4m3":
        byte = np.frexp(amax)[1] - 1 + 127 - 7
    else:
        mant, ex = np.frexp(amax / 6.0)
        byte = np.where(mant > 0.5, ex, ex - 1) + 127
    byte = np.clip(np.where(amax > 0, byte, 1), 1, 254)
    scaled = (w * np.exp2(127.0 - byte)[:, None, :]).reshape(k, n).astype(np.float32)
    by_word = np.ascontiguousarray(scaled.reshape(k // 512, 128, 4, n).transpose(0, 1, 3, 2))
    if fmt == "e4m3":
        words = by_word.astype(ml_dtypes.float8_e4m3fn).view(np.uint8)
    else:
        c = by_word.astype(ml_dtypes.float4_e2m1fn).view(np.uint8) & 0xF
        words = c[..., 0::2] | (c[..., 1::2] << 4)
    return np.ascontiguousarray(words), np.ascontiguousarray(byte.astype(np.uint8).reshape(k // 512, 16, n))


def unpack_weight(words, scales, fmt):
    g, p, n, _ = words.shape
    if fmt == "e4m3":
        vals = np.ascontiguousarray(words).view(ml_dtypes.float8_e4m3fn).astype(np.float64)
    else:
        nib = np.empty((g, p, n, 4), np.uint8)
        nib[..., 0::2] = words & 0xF
        nib[..., 1::2] = words >> 4
        vals = E2M1[nib]
    vals = vals * np.repeat(np.exp2(scales.astype(np.float64) - 127.0), 8, axis=1)[..., None]
    return vals.transpose(0, 1, 3, 2).reshape(g * 512, n)


B, I, H = 128, 8192, 512
FMT = "e4m3"


def sigmoid(v):
    return 1.0 / (1.0 + np.exp(-v))


def setup_inputs():
    s, u = mx_kscale(I), mx_kscale(H)
    t = np.random.uniform(0.5, 2.0, (B, 1)) * (np.random.random((B, 1)) >= 0.125)
    inp = bf(np.random.standard_normal((B, I)) * s)
    hx = bf(np.random.standard_normal((B, H)) * u)
    cx = bf(np.random.standard_normal((B, H)))
    ih_words, ih_scales = pack_weight((np.random.standard_normal((4 * H, I)) * 0.8 / np.sqrt(I) / s[None, :]).T, FMT)
    hh_words, hh_scales = pack_weight((np.random.standard_normal((4 * H, H)) * 0.8 / np.sqrt(H) / u[None, :]).T, FMT)
    bias_ih = bf(np.random.standard_normal(4 * H) * 0.4)
    bias_hh = bf(np.random.standard_normal(4 * H) * 0.4)
    wd_words, wd_scales = pack_weight(np.random.standard_normal((H, H)) / np.sqrt(H), FMT)
    b_decomp = bf(np.random.standard_normal(H) * 0.5)
    return {"input": inp,
            "t": bf(t),
            "hx": hx,
            "cx": cx,
            "weight_ih_words": ih_words,
            "weight_ih_scales": ih_scales,
            "weight_hh_words": hh_words,
            "weight_hh_scales": hh_scales,
            "bias_ih": bias_ih,
            "bias_hh": bias_hh,
            "W_decomp_words": wd_words,
            "W_decomp_scales": wd_scales,
            "b_decomp": b_decomp}


def reference(input, t, hx, cx, weight_ih_words, weight_ih_scales, weight_hh_words, weight_hh_scales, bias_ih, bias_hh, W_decomp_words, W_decomp_scales, b_decomp):
    W_decomp = unpack_weight(W_decomp_words, W_decomp_scales, FMT)
    H = W_decomp.shape[0]
    t = f64(t)
    cx = f64(cx)
    gates = ((mxq(f64(input), 1, "e4m3") @ unpack_weight(weight_ih_words, weight_ih_scales, FMT)) + f64(bias_ih)
             + (mxq(f64(hx), 1, "e4m3") @ unpack_weight(weight_hh_words, weight_hh_scales, FMT)) + f64(bias_hh))
    ingate, forgetgate, cellgate, outgate = np.split(gates, 4, axis=1)
    T = np.where(t != 0, 1.0 / np.where(t != 0, t, 1.0), 0.0)
    T = np.broadcast_to(T, (t.shape[0], H))
    C_ST = np.tanh((mxq(cx, 1, "e4m3") @ W_decomp) + f64(b_decomp))
    cx_adj = cx - C_ST + T * C_ST
    ingate = sigmoid(ingate)
    forgetgate = sigmoid(forgetgate)
    cellgate = np.tanh(cellgate)
    outgate = sigmoid(outgate)
    cy = forgetgate * cx_adj + ingate * cellgate
    hy = outgate * np.tanh(cy)
    return (hy, cy)

@@ -1,0 +1,248 @@
+import concourse.mybir as mybir
+from concourse.masks import make_identity
+
+FP8X4 = mybir.dt.float8_e4m3fn_x4
+BF16 = mybir.dt.bfloat16
+F32 = mybir.dt.float32
+I32 = mybir.dt.int32
+U32 = mybir.dt.uint32
+U8 = mybir.dt.uint8
+ACT = mybir.ActivationFunctionType
+ALU = mybir.AluOpType
+
+P = 128
+BATCH = 128
+IN = 8192
+H = 512
+GATES = 4
+GATE_I = 0
+GATE_F = 1
+GATE_G = 2
+GATE_O = 3
+K_PASS = 512
+IH_SLOTS = IN // K_PASS
+HH_SLOT = IH_SLOTS
+DC_SLOT = IH_SLOTS + 1
+SLOTS = IH_SLOTS + 2
+PAIRS_PER_SLOT = K_PASS // 2
+
+QUADRANT = 32
+QUADRANTS = P // QUADRANT
+PLANE_ROWS = 4
+PLANES_PER_BLOCK = 4
+PLANE_BLOCKS = (SLOTS + PLANES_PER_BLOCK - 1) // PLANES_PER_BLOCK
+
+TAIL_SLOTS = 4
+FIRST_TAIL_SLOT = IH_SLOTS - TAIL_SLOTS
+
+BIAS_COLS = GATES * H + H
+
+FLOPS = 2 * BATCH * (IN * GATES * H + H * GATES * H + H * H)
+
+
+def gate_columns(gate):
+    return slice(gate * H, (gate + 1) * H)
+
+
+def as_int32_words(packed):
+    return packed.rearrange("p n t -> p (n t)").bitcast(I32)
+
+
+def tile_ta_lstmcell_k_kernel(
+    tc,
+    inp,
+    t,
+    hx,
+    cx,
+    weight_ih_words,
+    weight_ih_scales,
+    weight_hh_words,
+    weight_hh_scales,
+    bias_ih,
+    bias_hh,
+    w_decomp_words,
+    w_decomp_scales,
+    b_decomp,
+    out_hy,
+    out_cy,
+):
+    nc = tc.nc
+    with tc.manual_schedule(), tc.tile_pool(name="keep", bufs=1) as keep, tc.tile_pool(
+        name="stage", bufs=3
+    ) as stage, tc.psum_pool(name="gates", bufs=1) as gates_psum, tc.psum_pool(name="work", bufs=4) as work:
+        acts = keep.tile([P, SLOTS * K_PASS], BF16)
+        act_codes = keep.tile([P, SLOTS * BATCH], U32, align_bytes=64)
+        act_scales = keep.tile([P, SLOTS * BATCH], U8, align_bytes=64)
+        w_ih = keep.tile([P, IH_SLOTS, GATES * H], U32, align_bytes=64)
+        w_hh = keep.tile([P, GATES * H], U32, align_bytes=64)
+        w_dc = keep.tile([P, H], U32, align_bytes=64)
+        planes = keep.tile([P, PLANE_BLOCKS, GATES * H], U8, align_bytes=64)
+        bias_rows = keep.tile([P, BIAS_COLS], BF16)
+        bias_all = keep.tile([P, BIAS_COLS], F32)
+        ones = keep.tile([P, P], BF16)
+        identity = keep.tile([P, P], F32)
+        t_sb = keep.tile([P, 1], BF16)
+        zero_col = keep.tile([P, 1], F32)
+        table_warm = keep.tile([P, 1], F32)
+
+        nc.vector.memset(bias_rows[:], 0.0)
+        nc.vector.memset(planes[:].rearrange("p a n -> p (a n)").bitcast(I32), 0)
+        nc.vector.memset(ones[:], 1.0)
+        nc.vector.memset(zero_col[:], 0.0)
+        make_identity(nc, identity[:])
+
+        nc.scalar.dma_start(out=acts[:, HH_SLOT * K_PASS : (HH_SLOT + 1) * K_PASS], in_=hx)
+        nc.scalar.dma_start(out=acts[:, DC_SLOT * K_PASS : (DC_SLOT + 1) * K_PASS], in_=cx)
+        nc.scalar.dma_start(out=t_sb[:], in_=t)
+        nc.scalar.dma_start(out=bias_rows[0:1, 0 : GATES * H], in_=bias_ih.unsqueeze(0))
+        nc.scalar.dma_start(out=bias_rows[1:2, 0 : GATES * H], in_=bias_hh.unsqueeze(0))
+        nc.scalar.dma_start(out=bias_rows[0:1, GATES * H : BIAS_COLS], in_=b_decomp.unsqueeze(0))
+
+        nc.scalar.activation(out=table_warm[:], in_=zero_col[:], func=ACT.Sigmoid)
+
+        def load_ih_plane_block(block):
+            first_slot = block * PLANES_PER_BLOCK
+            for quadrant in range(QUADRANTS):
+                first_partition = quadrant * QUADRANT
+                first_row = quadrant * PLANE_ROWS
+                nc.sync.dma_start(
+                    out=planes[first_partition : first_partition + PLANES_PER_BLOCK * PLANE_ROWS, block, :].bitcast(I32),
+                    in_=weight_ih_scales[
+                        first_slot : first_slot + PLANES_PER_BLOCK, first_row : first_row + PLANE_ROWS, :
+                    ].bitcast(I32),
+                )
+
+        def load_one_plane(slot, scales, width):
+            block = slot // PLANES_PER_BLOCK
+            for quadrant in range(QUADRANTS):
+                first_partition = quadrant * QUADRANT + (slot % PLANES_PER_BLOCK) * PLANE_ROWS
+                first_row = quadrant * PLANE_ROWS
+                nc.sync.dma_start(
+                    out=planes[first_partition : first_partition + PLANE_ROWS, block, 0:width].bitcast(I32),
+                    in_=scales[0, first_row : first_row + PLANE_ROWS, :].bitcast(I32),
+                )
+
+        for half in range(2):
+            columns = slice(half * IN // 2, (half + 1) * IN // 2)
+            nc.sync.dma_start(out=acts[:, columns], in_=inp[:, columns])
+
+        for slot in range(IH_SLOTS):
+            if slot % PLANES_PER_BLOCK == 0:
+                load_ih_plane_block(slot // PLANES_PER_BLOCK)
+            if slot < FIRST_TAIL_SLOT:
+                nc.sync.dma_start(out=w_ih[:, slot, :].bitcast(I32), in_=as_int32_words(weight_ih_words[slot]))
+            if slot == PLANES_PER_BLOCK - 1:
+                load_one_plane(HH_SLOT, weight_hh_scales, GATES * H)
+                nc.sync.dma_start(out=w_hh[:].bitcast(I32), in_=as_int32_words(weight_hh_words[0]))
+                load_one_plane(DC_SLOT, w_decomp_scales, H)
+                nc.sync.dma_start(out=w_dc[:].bitcast(I32), in_=as_int32_words(w_decomp_words[0]))
+        for gate in range(GATES):
+            for slot in range(FIRST_TAIL_SLOT, IH_SLOTS):
+                nc.sync.dma_start(
+                    out=w_ih[:, slot, gate_columns(gate)].bitcast(I32),
+                    in_=as_int32_words(weight_ih_words[slot])[:, gate_columns(gate)],
+                )
+
+        is_zero = keep.tile([P, 1], F32)
+        t_safe = keep.tile([P, 1], F32)
+        t_inverse = keep.tile([P, 1], F32)
+        t_minus_1 = keep.tile([P, 1], F32)
+        nc.vector.tensor_single_scalar(out=is_zero[:], in_=t_sb[:], scalar=0.0, op=ALU.is_equal)
+        nc.vector.tensor_tensor(out=t_safe[:], in0=t_sb[:], in1=is_zero[:], op=ALU.add)
+        nc.vector.reciprocal(out=t_inverse[:], in_=t_safe[:])
+        nc.vector.scalar_tensor_tensor(
+            out=t_minus_1[:], in0=t_inverse[:], scalar=-1.0, in1=is_zero[:], op0=ALU.add, op1=ALU.subtract
+        )
+
+        for chunk in range(BIAS_COLS // H):
+            columns = slice(chunk * H, (chunk + 1) * H)
+            bank = work.tile([P, H], F32)
+            nc.tensor.matmul(out=bank[:], lhsT=ones[:], rhs=bias_rows[:, columns], start=True, stop=True)
+            nc.vector.tensor_copy(out=bias_all[:, columns], in_=bank[:])
+
+        acts_pairs = acts[:].bitcast(F32)
+        for two_slots in range(SLOTS // 2):
+            bank = work.tile([P, H], F32)
+            for i in range(2):
+                slot = 2 * two_slots + i
+                for u in range(2):
+                    quarter = 2 * i + u
+                    nc.tensor.transpose(
+                        bank[:, quarter * BATCH : (quarter + 1) * BATCH],
+                        acts_pairs[:, slot * PAIRS_PER_SLOT + u : (slot + 1) * PAIRS_PER_SLOT : 2],
+                        identity[:],
+                    )
+            grouped = stage.tile([P, 2 * BATCH * 4], BF16, align_bytes=64)
+            nc.scalar.copy(
+                out=grouped[:].bitcast(F32).rearrange("p (i b u) -> p i b u", i=2, u=2),
+                in_=bank[:].rearrange("p (i u b) -> p i b u", i=2, u=2),
+            )
+            columns = slice(two_slots * 2 * BATCH, (two_slots + 1) * 2 * BATCH)
+            nc.vector.quantize_mx(
+                out=act_codes[:, columns].bitcast(FP8X4), scales=act_scales[:, columns], in_=grouped[:]
+            )
+
+        def mx_pass(out, slot, words, columns, start, stop):
+            rows = slice(slot * BATCH, (slot + 1) * BATCH)
+            first_partition = (slot % PLANES_PER_BLOCK) * PLANE_ROWS
+            nc.tensor.matmul_mx(
+                out=out,
+                lhsT=act_codes[:, rows].bitcast(FP8X4),
+                lhsT_scale=act_scales[:, rows],
+                rhs=words[:, columns].bitcast(FP8X4),
+                rhs_scale=planes[first_partition:P, slot // PLANES_PER_BLOCK, columns],
+                start=start,
+                stop=stop,
+            )
+
+        gate_sums = [gates_psum.tile([P, H], F32, name="gate_sum%d" % gate) for gate in range(GATES)]
+
+        for slot in range(FIRST_TAIL_SLOT):
+            for gate in range(GATES):
+                mx_pass(gate_sums[gate][:], slot, w_ih[:, slot, :], gate_columns(gate), start=(slot == 0), stop=False)
+            if slot == PLANES_PER_BLOCK - 1:
+                for gate in range(GATES):
+                    mx_pass(gate_sums[gate][:], HH_SLOT, w_hh[:], gate_columns(gate), start=False, stop=False)
+                bank = work.tile([P, H], F32)
+                mx_pass(bank[:], DC_SLOT, w_dc[:], slice(0, H), start=True, stop=True)
+                biased = stage.tile([P, H], F32)
+                nc.vector.tensor_tensor(out=biased[:], in0=bank[:], in1=bias_all[:, GATES * H : BIAS_COLS], op=ALU.add)
+                c_st = keep.tile([P, H], F32)
+                nc.scalar.activation(out=c_st[:], in_=biased[:], func=ACT.Tanh)
+                cx_adj = keep.tile([P, H], F32)
+                nc.vector.scalar_tensor_tensor(
+                    out=cx_adj[:],
+                    in0=c_st[:],
+                    scalar=t_minus_1[:, 0:1],
+                    in1=acts[:, DC_SLOT * K_PASS : (DC_SLOT + 1) * K_PASS],
+                    op0=ALU.mult,
+                    op1=ALU.add,
+                )
+
+        def finish_gate(gate, func):
+            for slot in range(FIRST_TAIL_SLOT, IH_SLOTS):
+                mx_pass(
+                    gate_sums[gate][:], slot, w_ih[:, slot, :], gate_columns(gate), start=False, stop=(slot == IH_SLOTS - 1)
+                )
+            biased = stage.tile([P, H], F32)
+            nc.vector.tensor_tensor(out=biased[:], in0=gate_sums[gate][:], in1=bias_all[:, gate_columns(gate)], op=ALU.add)
+            value = keep.tile([P, H], F32, name="gate_value%d" % gate)
+            nc.scalar.activation(out=value[:], in_=biased[:], func=func)
+            return value
+
+        sigmoid_i = finish_gate(GATE_I, ACT.Sigmoid)
+        sigmoid_f = finish_gate(GATE_F, ACT.Sigmoid)
+        kept = keep.tile([P, H], F32)
+        nc.vector.tensor_tensor(out=kept[:], in0=sigmoid_f[:], in1=cx_adj[:], op=ALU.mult)
+        tanh_g = finish_gate(GATE_G, ACT.Tanh)
+        fresh = keep.tile([P, H], F32)
+        nc.vector.tensor_tensor(out=fresh[:], in0=sigmoid_i[:], in1=tanh_g[:], op=ALU.mult)
+        cy = keep.tile([P, H], F32)
+        nc.vector.tensor_tensor(out=cy[:], in0=kept[:], in1=fresh[:], op=ALU.add)
+        nc.sync.dma_start(out=out_cy, in_=cy[:])
+        tanh_cy = keep.tile([P, H], F32)
+        nc.scalar.activation(out=tanh_cy[:], in_=cy[:], func=ACT.Tanh)
+        sigmoid_o = finish_gate(GATE_O, ACT.Sigmoid)
+        hy = keep.tile([P, H], F32)
+        nc.vector.tensor_tensor(out=hy[:], in0=sigmoid_o[:], in1=tanh_cy[:], op=ALU.mult)
+        nc.sync.dma_start(out=out_hy, in_=hy[:])

@@ -105,11 +105,11 @@ def tile_ta_lstmcell_k_kernel(
             for quadrant in range(QUADRANTS):
                 first_partition = quadrant * QUADRANT
                 first_row = quadrant * PLANE_ROWS
-                nc.sync.dma_start(
-                    out=planes[first_partition : first_partition + PLANES_PER_BLOCK * PLANE_ROWS, block, :].bitcast(I32),
+                nc.gpsimd.dma_start(
+                    out=planes[first_partition : first_partition + PLANES_PER_BLOCK * PLANE_ROWS, block, :].bitcast(F32),
                     in_=weight_ih_scales[
                         first_slot : first_slot + PLANES_PER_BLOCK, first_row : first_row + PLANE_ROWS, :
-                    ].bitcast(I32),
+                    ].bitcast(F32),
                 )
 
         def load_one_plane(slot, scales, width):
@@ -117,24 +117,25 @@ def tile_ta_lstmcell_k_kernel(
             for quadrant in range(QUADRANTS):
                 first_partition = quadrant * QUADRANT + (slot % PLANES_PER_BLOCK) * PLANE_ROWS
                 first_row = quadrant * PLANE_ROWS
-                nc.sync.dma_start(
-                    out=planes[first_partition : first_partition + PLANE_ROWS, block, 0:width].bitcast(I32),
-                    in_=scales[0, first_row : first_row + PLANE_ROWS, :].bitcast(I32),
+                nc.gpsimd.dma_start(
+                    out=planes[first_partition : first_partition + PLANE_ROWS, block, 0:width].bitcast(F32),
+                    in_=scales[0, first_row : first_row + PLANE_ROWS, :].bitcast(F32),
                 )
+
+        load_ih_plane_block(0)
+        load_one_plane(HH_SLOT, weight_hh_scales, GATES * H)
+        load_one_plane(DC_SLOT, w_decomp_scales, H)
+        for block in range(1, IH_SLOTS // PLANES_PER_BLOCK):
+            load_ih_plane_block(block)
 
         for half in range(2):
             columns = slice(half * IN // 2, (half + 1) * IN // 2)
             nc.sync.dma_start(out=acts[:, columns], in_=inp[:, columns])
 
-        for slot in range(IH_SLOTS):
-            if slot % PLANES_PER_BLOCK == 0:
-                load_ih_plane_block(slot // PLANES_PER_BLOCK)
-            if slot < FIRST_TAIL_SLOT:
-                nc.sync.dma_start(out=w_ih[:, slot, :].bitcast(I32), in_=as_int32_words(weight_ih_words[slot]))
+        for slot in range(FIRST_TAIL_SLOT):
+            nc.sync.dma_start(out=w_ih[:, slot, :].bitcast(I32), in_=as_int32_words(weight_ih_words[slot]))
             if slot == PLANES_PER_BLOCK - 1:
-                load_one_plane(HH_SLOT, weight_hh_scales, GATES * H)
                 nc.sync.dma_start(out=w_hh[:].bitcast(I32), in_=as_int32_words(weight_hh_words[0]))
-                load_one_plane(DC_SLOT, w_decomp_scales, H)
                 nc.sync.dma_start(out=w_dc[:].bitcast(I32), in_=as_int32_words(w_decomp_words[0]))
         for gate in range(GATES):
             for slot in range(FIRST_TAIL_SLOT, IH_SLOTS):

@@ -32,8 +32,10 @@ PLANE_ROWS = 4
 PLANES_PER_BLOCK = 4
 PLANE_BLOCKS = (SLOTS + PLANES_PER_BLOCK - 1) // PLANES_PER_BLOCK
 
-TAIL_SLOTS = 4
-FIRST_TAIL_SLOT = IH_SLOTS - TAIL_SLOTS
+EARLY_GATES = (GATE_I, GATE_F, GATE_G)
+EARLY_COLS = len(EARLY_GATES) * H
+
+SMALL_WEIGHTS_AFTER_SLOT = 7
 
 BIAS_COLS = GATES * H + H
 
@@ -85,8 +87,8 @@ def tile_ta_lstmcell_k_kernel(
         zero_col = keep.tile([P, 1], F32)
         table_warm = keep.tile([P, 1], F32)
 
-        nc.vector.memset(bias_rows[:], 0.0)
         nc.vector.memset(planes[:].rearrange("p a n -> p (a n)").bitcast(I32), 0)
+        nc.vector.memset(bias_rows[:], 0.0)
         nc.vector.memset(ones[:], 1.0)
         nc.vector.memset(zero_col[:], 0.0)
         make_identity(nc, identity[:])
@@ -122,27 +124,28 @@ def tile_ta_lstmcell_k_kernel(
                     in_=scales[0, first_row : first_row + PLANE_ROWS, :].bitcast(F32),
                 )
 
-        load_ih_plane_block(0)
-        load_one_plane(HH_SLOT, weight_hh_scales, GATES * H)
-        load_one_plane(DC_SLOT, w_decomp_scales, H)
-        for block in range(1, IH_SLOTS // PLANES_PER_BLOCK):
+        for block in range(IH_SLOTS // PLANES_PER_BLOCK):
             load_ih_plane_block(block)
+            if block == SMALL_WEIGHTS_AFTER_SLOT // PLANES_PER_BLOCK:
+                load_one_plane(HH_SLOT, weight_hh_scales, GATES * H)
+                load_one_plane(DC_SLOT, w_decomp_scales, H)
 
         for half in range(2):
             columns = slice(half * IN // 2, (half + 1) * IN // 2)
             nc.sync.dma_start(out=acts[:, columns], in_=inp[:, columns])
 
-        for slot in range(FIRST_TAIL_SLOT):
-            nc.sync.dma_start(out=w_ih[:, slot, :].bitcast(I32), in_=as_int32_words(weight_ih_words[slot]))
-            if slot == PLANES_PER_BLOCK - 1:
+        for slot in range(IH_SLOTS):
+            nc.sync.dma_start(
+                out=w_ih[:, slot, 0:EARLY_COLS].bitcast(I32), in_=as_int32_words(weight_ih_words[slot])[:, 0:EARLY_COLS]
+            )
+            if slot == SMALL_WEIGHTS_AFTER_SLOT:
                 nc.sync.dma_start(out=w_hh[:].bitcast(I32), in_=as_int32_words(weight_hh_words[0]))
                 nc.sync.dma_start(out=w_dc[:].bitcast(I32), in_=as_int32_words(w_decomp_words[0]))
-        for gate in range(GATES):
-            for slot in range(FIRST_TAIL_SLOT, IH_SLOTS):
-                nc.sync.dma_start(
-                    out=w_ih[:, slot, gate_columns(gate)].bitcast(I32),
-                    in_=as_int32_words(weight_ih_words[slot])[:, gate_columns(gate)],
-                )
+        for slot in range(IH_SLOTS):
+            nc.sync.dma_start(
+                out=w_ih[:, slot, gate_columns(GATE_O)].bitcast(I32),
+                in_=as_int32_words(weight_ih_words[slot])[:, gate_columns(GATE_O)],
+            )
 
         is_zero = keep.tile([P, 1], F32)
         t_safe = keep.tile([P, 1], F32)
@@ -198,12 +201,19 @@ def tile_ta_lstmcell_k_kernel(
 
         gate_sums = [gates_psum.tile([P, H], F32, name="gate_sum%d" % gate) for gate in range(GATES)]
 
-        for slot in range(FIRST_TAIL_SLOT):
-            for gate in range(GATES):
-                mx_pass(gate_sums[gate][:], slot, w_ih[:, slot, :], gate_columns(gate), start=(slot == 0), stop=False)
-            if slot == PLANES_PER_BLOCK - 1:
+        for slot in range(IH_SLOTS):
+            for gate in EARLY_GATES:
+                mx_pass(
+                    gate_sums[gate][:],
+                    slot,
+                    w_ih[:, slot, :],
+                    gate_columns(gate),
+                    start=(slot == 0),
+                    stop=(slot == IH_SLOTS - 1),
+                )
+            if slot == SMALL_WEIGHTS_AFTER_SLOT:
                 for gate in range(GATES):
-                    mx_pass(gate_sums[gate][:], HH_SLOT, w_hh[:], gate_columns(gate), start=False, stop=False)
+                    mx_pass(gate_sums[gate][:], HH_SLOT, w_hh[:], gate_columns(gate), start=(gate == GATE_O), stop=False)
                 bank = work.tile([P, H], F32)
                 mx_pass(bank[:], DC_SLOT, w_dc[:], slice(0, H), start=True, stop=True)
                 biased = stage.tile([P, H], F32)
@@ -221,10 +231,6 @@ def tile_ta_lstmcell_k_kernel(
                 )
 
         def finish_gate(gate, func):
-            for slot in range(FIRST_TAIL_SLOT, IH_SLOTS):
-                mx_pass(
-                    gate_sums[gate][:], slot, w_ih[:, slot, :], gate_columns(gate), start=False, stop=(slot == IH_SLOTS - 1)
-                )
             biased = stage.tile([P, H], F32)
             nc.vector.tensor_tensor(out=biased[:], in0=gate_sums[gate][:], in1=bias_all[:, gate_columns(gate)], op=ALU.add)
             value = keep.tile([P, H], F32, name="gate_value%d" % gate)
@@ -243,6 +249,11 @@ def tile_ta_lstmcell_k_kernel(
         nc.sync.dma_start(out=out_cy, in_=cy[:])
         tanh_cy = keep.tile([P, H], F32)
         nc.scalar.activation(out=tanh_cy[:], in_=cy[:], func=ACT.Tanh)
+
+        for slot in range(IH_SLOTS):
+            mx_pass(
+                gate_sums[GATE_O][:], slot, w_ih[:, slot, :], gate_columns(GATE_O), start=False, stop=(slot == IH_SLOTS - 1)
+            )
         sigmoid_o = finish_gate(GATE_O, ACT.Sigmoid)
         hy = keep.tile([P, H], F32)
         nc.vector.tensor_tensor(out=hy[:], in0=sigmoid_o[:], in1=tanh_cy[:], op=ALU.mult)

@@ -254,7 +254,16 @@ def tile_ta_lstmcell_k_kernel(
             mx_pass(
                 gate_sums[GATE_O][:], slot, w_ih[:, slot, :], gate_columns(GATE_O), start=False, stop=(slot == IH_SLOTS - 1)
             )
-        sigmoid_o = finish_gate(GATE_O, ACT.Sigmoid)
+        halves = [slice(half * H // 2, (half + 1) * H // 2) for half in range(2)]
+        bias_o = bias_all[:, gate_columns(GATE_O)]
+        biased_o = keep.tile([P, H], F32)
+        sigmoid_o = keep.tile([P, H], F32)
         hy = keep.tile([P, H], F32)
-        nc.vector.tensor_tensor(out=hy[:], in0=sigmoid_o[:], in1=tanh_cy[:], op=ALU.mult)
-        nc.sync.dma_start(out=out_hy, in_=hy[:])
+        for columns in halves:
+            nc.vector.tensor_tensor(
+                out=biased_o[:, columns], in0=gate_sums[GATE_O][:, columns], in1=bias_o[:, columns], op=ALU.add
+            )
+            nc.scalar.activation(out=sigmoid_o[:, columns], in_=biased_o[:, columns], func=ACT.Sigmoid)
+        for columns in halves:
+            nc.vector.tensor_tensor(out=hy[:, columns], in0=sigmoid_o[:, columns], in1=tanh_cy[:, columns], op=ALU.mult)
+            nc.sync.dma_start(out=out_hy[:, columns], in_=hy[:, columns])

@@ -114,21 +114,17 @@ def tile_ta_lstmcell_k_kernel(
                     ].bitcast(F32),
                 )
 
-        def load_one_plane(slot, scales, width):
+        def load_plane_quadrant(slot, scales, width, quadrant):
             block = slot // PLANES_PER_BLOCK
-            for quadrant in range(QUADRANTS):
-                first_partition = quadrant * QUADRANT + (slot % PLANES_PER_BLOCK) * PLANE_ROWS
-                first_row = quadrant * PLANE_ROWS
-                nc.gpsimd.dma_start(
-                    out=planes[first_partition : first_partition + PLANE_ROWS, block, 0:width].bitcast(F32),
-                    in_=scales[0, first_row : first_row + PLANE_ROWS, :].bitcast(F32),
-                )
+            first_partition = quadrant * QUADRANT + (slot % PLANES_PER_BLOCK) * PLANE_ROWS
+            first_row = quadrant * PLANE_ROWS
+            nc.sync.dma_start(
+                out=planes[first_partition : first_partition + PLANE_ROWS, block, 0:width].bitcast(I32),
+                in_=scales[0, first_row : first_row + PLANE_ROWS, :].bitcast(I32),
+            )
 
         for block in range(IH_SLOTS // PLANES_PER_BLOCK):
             load_ih_plane_block(block)
-            if block == SMALL_WEIGHTS_AFTER_SLOT // PLANES_PER_BLOCK:
-                load_one_plane(HH_SLOT, weight_hh_scales, GATES * H)
-                load_one_plane(DC_SLOT, w_decomp_scales, H)
 
         for half in range(2):
             columns = slice(half * IN // 2, (half + 1) * IN // 2)
@@ -138,6 +134,10 @@ def tile_ta_lstmcell_k_kernel(
             nc.sync.dma_start(
                 out=w_ih[:, slot, 0:EARLY_COLS].bitcast(I32), in_=as_int32_words(weight_ih_words[slot])[:, 0:EARLY_COLS]
             )
+            if slot < QUADRANTS:
+                load_plane_quadrant(HH_SLOT, weight_hh_scales, GATES * H, slot)
+            elif slot < 2 * QUADRANTS:
+                load_plane_quadrant(DC_SLOT, w_decomp_scales, H, slot - QUADRANTS)
             if slot == SMALL_WEIGHTS_AFTER_SLOT:
                 nc.sync.dma_start(out=w_hh[:].bitcast(I32), in_=as_int32_words(weight_hh_words[0]))
                 nc.sync.dma_start(out=w_dc[:].bitcast(I32), in_=as_int32_words(w_decomp_words[0]))

@@ -35,6 +35,8 @@ PLANE_BLOCKS = (SLOTS + PLANES_PER_BLOCK - 1) // PLANES_PER_BLOCK
 EARLY_GATES = (GATE_I, GATE_F, GATE_G)
 EARLY_COLS = len(EARLY_GATES) * H
 
+WHOLE_SLOTS = 8
+
 SMALL_WEIGHTS_AFTER_SLOT = 7
 
 BIAS_COLS = GATES * H + H
@@ -131,8 +133,9 @@ def tile_ta_lstmcell_k_kernel(
             nc.sync.dma_start(out=acts[:, columns], in_=inp[:, columns])
 
         for slot in range(IH_SLOTS):
+            width = GATES * H if slot < WHOLE_SLOTS else EARLY_COLS
             nc.sync.dma_start(
-                out=w_ih[:, slot, 0:EARLY_COLS].bitcast(I32), in_=as_int32_words(weight_ih_words[slot])[:, 0:EARLY_COLS]
+                out=w_ih[:, slot, 0:width].bitcast(I32), in_=as_int32_words(weight_ih_words[slot])[:, 0:width]
             )
             if slot < QUADRANTS:
                 load_plane_quadrant(HH_SLOT, weight_hh_scales, GATES * H, slot)
@@ -141,7 +144,7 @@ def tile_ta_lstmcell_k_kernel(
             if slot == SMALL_WEIGHTS_AFTER_SLOT:
                 nc.sync.dma_start(out=w_hh[:].bitcast(I32), in_=as_int32_words(weight_hh_words[0]))
                 nc.sync.dma_start(out=w_dc[:].bitcast(I32), in_=as_int32_words(w_decomp_words[0]))
-        for slot in range(IH_SLOTS):
+        for slot in range(WHOLE_SLOTS, IH_SLOTS):
             nc.sync.dma_start(
                 out=w_ih[:, slot, gate_columns(GATE_O)].bitcast(I32),
                 in_=as_int32_words(weight_ih_words[slot])[:, gate_columns(GATE_O)],
@@ -211,9 +214,11 @@ def tile_ta_lstmcell_k_kernel(
                     start=(slot == 0),
                     stop=(slot == IH_SLOTS - 1),
                 )
+            if slot < WHOLE_SLOTS:
+                mx_pass(gate_sums[GATE_O][:], slot, w_ih[:, slot, :], gate_columns(GATE_O), start=(slot == 0), stop=False)
             if slot == SMALL_WEIGHTS_AFTER_SLOT:
                 for gate in range(GATES):
-                    mx_pass(gate_sums[gate][:], HH_SLOT, w_hh[:], gate_columns(gate), start=(gate == GATE_O), stop=False)
+                    mx_pass(gate_sums[gate][:], HH_SLOT, w_hh[:], gate_columns(gate), start=False, stop=False)
                 bank = work.tile([P, H], F32)
                 mx_pass(bank[:], DC_SLOT, w_dc[:], slice(0, H), start=True, stop=True)
                 biased = stage.tile([P, H], F32)
@@ -239,9 +244,9 @@ def tile_ta_lstmcell_k_kernel(
 
         sigmoid_i = finish_gate(GATE_I, ACT.Sigmoid)
         sigmoid_f = finish_gate(GATE_F, ACT.Sigmoid)
+        tanh_g = finish_gate(GATE_G, ACT.Tanh)
         kept = keep.tile([P, H], F32)
         nc.vector.tensor_tensor(out=kept[:], in0=sigmoid_f[:], in1=cx_adj[:], op=ALU.mult)
-        tanh_g = finish_gate(GATE_G, ACT.Tanh)
         fresh = keep.tile([P, H], F32)
         nc.vector.tensor_tensor(out=fresh[:], in0=sigmoid_i[:], in1=tanh_g[:], op=ALU.mult)
         cy = keep.tile([P, H], F32)
@@ -250,7 +255,7 @@ def tile_ta_lstmcell_k_kernel(
         tanh_cy = keep.tile([P, H], F32)
         nc.scalar.activation(out=tanh_cy[:], in_=cy[:], func=ACT.Tanh)
 
-        for slot in range(IH_SLOTS):
+        for slot in range(WHOLE_SLOTS, IH_SLOTS):
             mx_pass(
                 gate_sums[GATE_O][:], slot, w_ih[:, slot, :], gate_columns(GATE_O), start=False, stop=(slot == IH_SLOTS - 1)
             )

@@ -19,6 +19,7 @@ GATE_I = 0
 GATE_F = 1
 GATE_G = 2
 GATE_O = 3
+HALF = H // 2
 K_PASS = 512
 IH_SLOTS = IN // K_PASS
 HH_SLOT = IH_SLOTS
@@ -73,7 +74,9 @@ def tile_ta_lstmcell_k_kernel(
     nc = tc.nc
     with tc.manual_schedule(), tc.tile_pool(name="keep", bufs=1) as keep, tc.tile_pool(
         name="stage", bufs=3
-    ) as stage, tc.psum_pool(name="gates", bufs=1) as gates_psum, tc.psum_pool(name="work", bufs=4) as work:
+    ) as stage, tc.psum_pool(name="gates", bufs=1) as gates_psum, tc.psum_pool(name="work", bufs=3) as work:
+        o_halves = [slice(GATE_O * H + half * HALF, GATE_O * H + (half + 1) * HALF) for half in range(2)]
+
         acts = keep.tile([P, SLOTS * K_PASS], BF16)
         act_codes = keep.tile([P, SLOTS * BATCH], U32, align_bytes=64)
         act_scales = keep.tile([P, SLOTS * BATCH], U8, align_bytes=64)
@@ -145,10 +148,11 @@ def tile_ta_lstmcell_k_kernel(
                 nc.sync.dma_start(out=w_hh[:].bitcast(I32), in_=as_int32_words(weight_hh_words[0]))
                 nc.sync.dma_start(out=w_dc[:].bitcast(I32), in_=as_int32_words(w_decomp_words[0]))
         for slot in range(WHOLE_SLOTS, IH_SLOTS):
-            nc.sync.dma_start(
-                out=w_ih[:, slot, gate_columns(GATE_O)].bitcast(I32),
-                in_=as_int32_words(weight_ih_words[slot])[:, gate_columns(GATE_O)],
-            )
+            pieces = o_halves if slot == IH_SLOTS - 1 else [gate_columns(GATE_O)]
+            for columns in pieces:
+                nc.sync.dma_start(
+                    out=w_ih[:, slot, columns].bitcast(I32), in_=as_int32_words(weight_ih_words[slot])[:, columns]
+                )
 
         is_zero = keep.tile([P, 1], F32)
         t_safe = keep.tile([P, 1], F32)
@@ -202,7 +206,12 @@ def tile_ta_lstmcell_k_kernel(
                 stop=stop,
             )
 
-        gate_sums = [gates_psum.tile([P, H], F32, name="gate_sum%d" % gate) for gate in range(GATES)]
+        gate_sums = [gates_psum.tile([P, H], F32, name="gate_sum%d" % gate) for gate in EARLY_GATES]
+        o_sums = [gates_psum.tile([P, HALF], F32, name="o_sum%d" % half) for half in range(2)]
+
+        def o_passes(slot, words, start, stop):
+            for half in range(2):
+                mx_pass(o_sums[half][:], slot, words, o_halves[half], start=start, stop=stop)
 
         for slot in range(IH_SLOTS):
             for gate in EARLY_GATES:
@@ -215,10 +224,11 @@ def tile_ta_lstmcell_k_kernel(
                     stop=(slot == IH_SLOTS - 1),
                 )
             if slot < WHOLE_SLOTS:
-                mx_pass(gate_sums[GATE_O][:], slot, w_ih[:, slot, :], gate_columns(GATE_O), start=(slot == 0), stop=False)
+                o_passes(slot, w_ih[:, slot, :], start=(slot == 0), stop=False)
             if slot == SMALL_WEIGHTS_AFTER_SLOT:
-                for gate in range(GATES):
+                for gate in EARLY_GATES:
                     mx_pass(gate_sums[gate][:], HH_SLOT, w_hh[:], gate_columns(gate), start=False, stop=False)
+                o_passes(HH_SLOT, w_hh[:], start=False, stop=False)
                 bank = work.tile([P, H], F32)
                 mx_pass(bank[:], DC_SLOT, w_dc[:], slice(0, H), start=True, stop=True)
                 biased = stage.tile([P, H], F32)
@@ -256,18 +266,14 @@ def tile_ta_lstmcell_k_kernel(
         nc.scalar.activation(out=tanh_cy[:], in_=cy[:], func=ACT.Tanh)
 
         for slot in range(WHOLE_SLOTS, IH_SLOTS):
-            mx_pass(
-                gate_sums[GATE_O][:], slot, w_ih[:, slot, :], gate_columns(GATE_O), start=False, stop=(slot == IH_SLOTS - 1)
-            )
+            o_passes(slot, w_ih[:, slot, :], start=False, stop=(slot == IH_SLOTS - 1))
         halves = [slice(half * H // 2, (half + 1) * H // 2) for half in range(2)]
         bias_o = bias_all[:, gate_columns(GATE_O)]
         biased_o = keep.tile([P, H], F32)
         sigmoid_o = keep.tile([P, H], F32)
         hy = keep.tile([P, H], F32)
-        for columns in halves:
-            nc.vector.tensor_tensor(
-                out=biased_o[:, columns], in0=gate_sums[GATE_O][:, columns], in1=bias_o[:, columns], op=ALU.add
-            )
+        for half, columns in enumerate(halves):
+            nc.vector.tensor_tensor(out=biased_o[:, columns], in0=o_sums[half][:], in1=bias_o[:, columns], op=ALU.add)
             nc.scalar.activation(out=sigmoid_o[:, columns], in_=biased_o[:, columns], func=ACT.Sigmoid)
         for columns in halves:
             nc.vector.tensor_tensor(out=hy[:, columns], in0=sigmoid_o[:, columns], in1=tanh_cy[:, columns], op=ALU.mult)

@@ -84,11 +84,11 @@ def tile_ta_lstmcell_k_kernel(
         w_hh = keep.tile([P, GATES * H], U32, align_bytes=64)
         w_dc = keep.tile([P, H], U32, align_bytes=64)
         planes = keep.tile([P, PLANE_BLOCKS, GATES * H], U8, align_bytes=64)
-        bias_rows = keep.tile([P, BIAS_COLS], BF16)
+        bias_rows = keep.tile([P, BIAS_COLS + BATCH], BF16)
         bias_all = keep.tile([P, BIAS_COLS], F32)
         ones = keep.tile([P, P], BF16)
         identity = keep.tile([P, P], F32)
-        t_sb = keep.tile([P, 1], BF16)
+        t_sb = keep.tile([P, 1], F32)
         zero_col = keep.tile([P, 1], F32)
         table_warm = keep.tile([P, 1], F32)
 
@@ -100,7 +100,7 @@ def tile_ta_lstmcell_k_kernel(
 
         nc.scalar.dma_start(out=acts[:, HH_SLOT * K_PASS : (HH_SLOT + 1) * K_PASS], in_=hx)
         nc.scalar.dma_start(out=acts[:, DC_SLOT * K_PASS : (DC_SLOT + 1) * K_PASS], in_=cx)
-        nc.scalar.dma_start(out=t_sb[:], in_=t)
+        nc.scalar.dma_start(out=bias_rows[0:1, BIAS_COLS : BIAS_COLS + BATCH], in_=t.rearrange("b one -> one b"))
         nc.scalar.dma_start(out=bias_rows[0:1, 0 : GATES * H], in_=bias_ih.unsqueeze(0))
         nc.scalar.dma_start(out=bias_rows[1:2, 0 : GATES * H], in_=bias_hh.unsqueeze(0))
         nc.scalar.dma_start(out=bias_rows[0:1, GATES * H : BIAS_COLS], in_=b_decomp.unsqueeze(0))
@@ -158,6 +158,11 @@ def tile_ta_lstmcell_k_kernel(
         t_safe = keep.tile([P, 1], F32)
         t_inverse = keep.tile([P, 1], F32)
         t_minus_1 = keep.tile([P, 1], F32)
+        bank = work.tile([P, H], F32)
+        nc.tensor.matmul(
+            out=bank[:, 0:1], lhsT=bias_rows[:, BIAS_COLS : BIAS_COLS + BATCH], rhs=ones[:, 0:1], start=True, stop=True
+        )
+        nc.vector.tensor_copy(out=t_sb[:], in_=bank[:, 0:1])
         nc.vector.tensor_single_scalar(out=is_zero[:], in_=t_sb[:], scalar=0.0, op=ALU.is_equal)
         nc.vector.tensor_tensor(out=t_safe[:], in0=t_sb[:], in1=is_zero[:], op=ALU.add)
         nc.vector.reciprocal(out=t_inverse[:], in_=t_safe[:])

@@ -31,7 +31,8 @@ QUADRANT = 32
 QUADRANTS = P // QUADRANT
 PLANE_ROWS = 4
 PLANES_PER_BLOCK = 4
-PLANE_BLOCKS = (SLOTS + PLANES_PER_BLOCK - 1) // PLANES_PER_BLOCK
+SMALL_BLOCK = IH_SLOTS // PLANES_PER_BLOCK
+PLANE_BLOCKS = SMALL_BLOCK + 1
 
 EARLY_GATES = (GATE_I, GATE_F, GATE_G)
 EARLY_COLS = len(EARLY_GATES) * H
@@ -100,10 +101,10 @@ def tile_ta_lstmcell_k_kernel(
 
         nc.scalar.dma_start(out=acts[:, HH_SLOT * K_PASS : (HH_SLOT + 1) * K_PASS], in_=hx)
         nc.scalar.dma_start(out=acts[:, DC_SLOT * K_PASS : (DC_SLOT + 1) * K_PASS], in_=cx)
-        nc.scalar.dma_start(out=bias_rows[0:1, BIAS_COLS : BIAS_COLS + BATCH], in_=t.rearrange("b one -> one b"))
-        nc.scalar.dma_start(out=bias_rows[0:1, 0 : GATES * H], in_=bias_ih.unsqueeze(0))
-        nc.scalar.dma_start(out=bias_rows[1:2, 0 : GATES * H], in_=bias_hh.unsqueeze(0))
-        nc.scalar.dma_start(out=bias_rows[0:1, GATES * H : BIAS_COLS], in_=b_decomp.unsqueeze(0))
+        nc.scalar.dma_start(out=bias_rows[16:17, BIAS_COLS : BIAS_COLS + BATCH], in_=t.rearrange("b one -> one b"))
+        nc.scalar.dma_start(out=bias_rows[20:21, 0 : GATES * H], in_=bias_ih.unsqueeze(0))
+        nc.scalar.dma_start(out=bias_rows[24:25, 0 : GATES * H], in_=bias_hh.unsqueeze(0))
+        nc.scalar.dma_start(out=bias_rows[28:29, GATES * H : BIAS_COLS], in_=b_decomp.unsqueeze(0))
 
         nc.scalar.activation(out=table_warm[:], in_=zero_col[:], func=ACT.Sigmoid)
 
@@ -119,13 +120,22 @@ def tile_ta_lstmcell_k_kernel(
                     ].bitcast(F32),
                 )
 
-        def load_plane_quadrant(slot, scales, width, quadrant):
-            block = slot // PLANES_PER_BLOCK
-            first_partition = quadrant * QUADRANT + (slot % PLANES_PER_BLOCK) * PLANE_ROWS
+        def load_hh_planes(quadrant):
+            first_partition = quadrant * QUADRANT
             first_row = quadrant * PLANE_ROWS
             nc.sync.dma_start(
-                out=planes[first_partition : first_partition + PLANE_ROWS, block, 0:width].bitcast(I32),
-                in_=scales[0, first_row : first_row + PLANE_ROWS, :].bitcast(I32),
+                out=planes[first_partition : first_partition + GATES * PLANE_ROWS, SMALL_BLOCK, 0:H].bitcast(I32),
+                in_=weight_hh_scales[0, first_row : first_row + PLANE_ROWS, :]
+                .rearrange("r (c n) -> c r n", c=GATES)
+                .bitcast(I32),
+            )
+
+        def load_dc_plane(quadrant):
+            first_partition = quadrant * QUADRANT
+            first_row = quadrant * PLANE_ROWS
+            nc.sync.dma_start(
+                out=planes[first_partition : first_partition + PLANE_ROWS, SMALL_BLOCK, H : 2 * H].bitcast(I32),
+                in_=w_decomp_scales[0, first_row : first_row + PLANE_ROWS, :].bitcast(I32),
             )
 
         for block in range(IH_SLOTS // PLANES_PER_BLOCK):
@@ -141,9 +151,9 @@ def tile_ta_lstmcell_k_kernel(
                 out=w_ih[:, slot, 0:width].bitcast(I32), in_=as_int32_words(weight_ih_words[slot])[:, 0:width]
             )
             if slot < QUADRANTS:
-                load_plane_quadrant(HH_SLOT, weight_hh_scales, GATES * H, slot)
+                load_hh_planes(slot)
             elif slot < 2 * QUADRANTS:
-                load_plane_quadrant(DC_SLOT, w_decomp_scales, H, slot - QUADRANTS)
+                load_dc_plane(slot - QUADRANTS)
             if slot == SMALL_WEIGHTS_AFTER_SLOT:
                 nc.sync.dma_start(out=w_hh[:].bitcast(I32), in_=as_int32_words(weight_hh_words[0]))
                 nc.sync.dma_start(out=w_dc[:].bitcast(I32), in_=as_int32_words(w_decomp_words[0]))
@@ -200,13 +210,19 @@ def tile_ta_lstmcell_k_kernel(
 
         def mx_pass(out, slot, words, columns, start, stop):
             rows = slice(slot * BATCH, (slot + 1) * BATCH)
-            first_partition = (slot % PLANES_PER_BLOCK) * PLANE_ROWS
+            if slot == HH_SLOT:
+                gate = columns.start // H
+                plane = planes[gate * PLANE_ROWS : P, SMALL_BLOCK, columns.start - gate * H : columns.stop - gate * H]
+            elif slot == DC_SLOT:
+                plane = planes[0:P, SMALL_BLOCK, H + columns.start : H + columns.stop]
+            else:
+                plane = planes[(slot % PLANES_PER_BLOCK) * PLANE_ROWS : P, slot // PLANES_PER_BLOCK, columns]
             nc.tensor.matmul_mx(
                 out=out,
                 lhsT=act_codes[:, rows].bitcast(FP8X4),
                 lhsT_scale=act_scales[:, rows],
                 rhs=words[:, columns].bitcast(FP8X4),
-                rhs_scale=planes[first_partition:P, slot // PLANES_PER_BLOCK, columns],
+                rhs_scale=plane,
                 start=start,
                 stop=stop,
             )

import concourse.mybir as mybir
from concourse.masks import make_identity

FP8X4 = mybir.dt.float8_e4m3fn_x4
BF16 = mybir.dt.bfloat16
F32 = mybir.dt.float32
I32 = mybir.dt.int32
U32 = mybir.dt.uint32
U8 = mybir.dt.uint8
ACT = mybir.ActivationFunctionType
ALU = mybir.AluOpType

P = 128
BATCH = 128
IN = 8192
H = 512
GATES = 4
GATE_I = 0
GATE_F = 1
GATE_G = 2
GATE_O = 3
HALF = H // 2
K_PASS = 512
IH_SLOTS = IN // K_PASS
HH_SLOT = IH_SLOTS
DC_SLOT = IH_SLOTS + 1
SLOTS = IH_SLOTS + 2
PAIRS_PER_SLOT = K_PASS // 2

QUADRANT = 32
QUADRANTS = P // QUADRANT
PLANE_ROWS = 4
PLANES_PER_BLOCK = 4
SMALL_BLOCK = IH_SLOTS // PLANES_PER_BLOCK
PLANE_BLOCKS = SMALL_BLOCK + 1

EARLY_GATES = (GATE_I, GATE_F, GATE_G)
EARLY_COLS = len(EARLY_GATES) * H

WHOLE_SLOTS = 8

SMALL_WEIGHTS_AFTER_SLOT = 7

BIAS_COLS = GATES * H + H

FLOPS = 2 * BATCH * (IN * GATES * H + H * GATES * H + H * H)


def gate_columns(gate):
    return slice(gate * H, (gate + 1) * H)


def as_int32_words(packed):
    return packed.rearrange("p n t -> p (n t)").bitcast(I32)


def tile_ta_lstmcell_k_kernel(
    tc,
    inp,
    t,
    hx,
    cx,
    weight_ih_words,
    weight_ih_scales,
    weight_hh_words,
    weight_hh_scales,
    bias_ih,
    bias_hh,
    w_decomp_words,
    w_decomp_scales,
    b_decomp,
    out_hy,
    out_cy,
):
    nc = tc.nc
    with tc.manual_schedule(), tc.tile_pool(name="keep", bufs=1) as keep, tc.tile_pool(
        name="stage", bufs=3
    ) as stage, tc.psum_pool(name="gates", bufs=1) as gates_psum, tc.psum_pool(name="work", bufs=3) as work:
        o_halves = [slice(GATE_O * H + half * HALF, GATE_O * H + (half + 1) * HALF) for half in range(2)]

        acts = keep.tile([P, SLOTS * K_PASS], BF16)
        act_codes = keep.tile([P, SLOTS * BATCH], U32, align_bytes=64)
        act_scales = keep.tile([P, SLOTS * BATCH], U8, align_bytes=64)
        w_ih = keep.tile([P, IH_SLOTS, GATES * H], U32, align_bytes=64)
        w_hh = keep.tile([P, GATES * H], U32, align_bytes=64)
        w_dc = keep.tile([P, H], U32, align_bytes=64)
        planes = keep.tile([P, PLANE_BLOCKS, GATES * H], U8, align_bytes=64)
        bias_rows = keep.tile([P, BIAS_COLS + BATCH], BF16)
        bias_all = keep.tile([P, BIAS_COLS], F32)
        ones = keep.tile([P, P], BF16)
        identity = keep.tile([P, P], F32)
        t_sb = keep.tile([P, 1], F32)
        zero_col = keep.tile([P, 1], F32)
        table_warm = keep.tile([P, 1], F32)

        nc.vector.memset(planes[:].rearrange("p a n -> p (a n)").bitcast(I32), 0)
        nc.vector.memset(bias_rows[:], 0.0)
        nc.vector.memset(ones[:], 1.0)
        nc.vector.memset(zero_col[:], 0.0)
        make_identity(nc, identity[:])

        nc.scalar.dma_start(out=acts[:, HH_SLOT * K_PASS : (HH_SLOT + 1) * K_PASS], in_=hx)
        nc.scalar.dma_start(out=acts[:, DC_SLOT * K_PASS : (DC_SLOT + 1) * K_PASS], in_=cx)
        nc.scalar.dma_start(out=bias_rows[16:17, BIAS_COLS : BIAS_COLS + BATCH], in_=t.rearrange("b one -> one b"))
        nc.scalar.dma_start(out=bias_rows[20:21, 0 : GATES * H], in_=bias_ih.unsqueeze(0))
        nc.scalar.dma_start(out=bias_rows[24:25, 0 : GATES * H], in_=bias_hh.unsqueeze(0))
        nc.scalar.dma_start(out=bias_rows[28:29, GATES * H : BIAS_COLS], in_=b_decomp.unsqueeze(0))

        nc.scalar.activation(out=table_warm[:], in_=zero_col[:], func=ACT.Sigmoid)

        def load_ih_plane_block(block):
            first_slot = block * PLANES_PER_BLOCK
            for quadrant in range(QUADRANTS):
                first_partition = quadrant * QUADRANT
                first_row = quadrant * PLANE_ROWS
                nc.gpsimd.dma_start(
                    out=planes[first_partition : first_partition + PLANES_PER_BLOCK * PLANE_ROWS, block, :].bitcast(F32),
                    in_=weight_ih_scales[
                        first_slot : first_slot + PLANES_PER_BLOCK, first_row : first_row + PLANE_ROWS, :
                    ].bitcast(F32),
                )

        def load_hh_planes(quadrant):
            first_partition = quadrant * QUADRANT
            first_row = quadrant * PLANE_ROWS
            nc.sync.dma_start(
                out=planes[first_partition : first_partition + GATES * PLANE_ROWS, SMALL_BLOCK, 0:H].bitcast(I32),
                in_=weight_hh_scales[0, first_row : first_row + PLANE_ROWS, :]
                .rearrange("r (c n) -> c r n", c=GATES)
                .bitcast(I32),
            )

        def load_dc_plane(quadrant):
            first_partition = quadrant * QUADRANT
            first_row = quadrant * PLANE_ROWS
            nc.sync.dma_start(
                out=planes[first_partition : first_partition + PLANE_ROWS, SMALL_BLOCK, H : 2 * H].bitcast(I32),
                in_=w_decomp_scales[0, first_row : first_row + PLANE_ROWS, :].bitcast(I32),
            )

        for block in range(IH_SLOTS // PLANES_PER_BLOCK):
            load_ih_plane_block(block)

        for half in range(2):
            columns = slice(half * IN // 2, (half + 1) * IN // 2)
            nc.sync.dma_start(out=acts[:, columns], in_=inp[:, columns])

        for slot in range(IH_SLOTS):
            width = GATES * H if slot < WHOLE_SLOTS else EARLY_COLS
            nc.sync.dma_start(
                out=w_ih[:, slot, 0:width].bitcast(I32), in_=as_int32_words(weight_ih_words[slot])[:, 0:width]
            )
            if slot < QUADRANTS:
                load_hh_planes(slot)
            elif slot < 2 * QUADRANTS:
                load_dc_plane(slot - QUADRANTS)
            if slot == SMALL_WEIGHTS_AFTER_SLOT:
                nc.sync.dma_start(out=w_hh[:].bitcast(I32), in_=as_int32_words(weight_hh_words[0]))
                nc.sync.dma_start(out=w_dc[:].bitcast(I32), in_=as_int32_words(w_decomp_words[0]))
        for slot in range(WHOLE_SLOTS, IH_SLOTS):
            pieces = o_halves if slot == IH_SLOTS - 1 else [gate_columns(GATE_O)]
            for columns in pieces:
                nc.sync.dma_start(
                    out=w_ih[:, slot, columns].bitcast(I32), in_=as_int32_words(weight_ih_words[slot])[:, columns]
                )

        is_zero = keep.tile([P, 1], F32)
        t_safe = keep.tile([P, 1], F32)
        t_inverse = keep.tile([P, 1], F32)
        t_minus_1 = keep.tile([P, 1], F32)
        bank = work.tile([P, H], F32)
        nc.tensor.matmul(
            out=bank[:, 0:1], lhsT=bias_rows[:, BIAS_COLS : BIAS_COLS + BATCH], rhs=ones[:, 0:1], start=True, stop=True
        )
        nc.vector.tensor_copy(out=t_sb[:], in_=bank[:, 0:1])
        nc.vector.tensor_single_scalar(out=is_zero[:], in_=t_sb[:], scalar=0.0, op=ALU.is_equal)
        nc.vector.tensor_tensor(out=t_safe[:], in0=t_sb[:], in1=is_zero[:], op=ALU.add)
        nc.vector.reciprocal(out=t_inverse[:], in_=t_safe[:])
        nc.vector.scalar_tensor_tensor(
            out=t_minus_1[:], in0=t_inverse[:], scalar=-1.0, in1=is_zero[:], op0=ALU.add, op1=ALU.subtract
        )

        for chunk in range(BIAS_COLS // H):
            columns = slice(chunk * H, (chunk + 1) * H)
            bank = work.tile([P, H], F32)
            nc.tensor.matmul(out=bank[:], lhsT=ones[:], rhs=bias_rows[:, columns], start=True, stop=True)
            nc.vector.tensor_copy(out=bias_all[:, columns], in_=bank[:])

        acts_pairs = acts[:].bitcast(F32)
        for two_slots in range(SLOTS // 2):
            bank = work.tile([P, H], F32)
            for i in range(2):
                slot = 2 * two_slots + i
                for u in range(2):
                    quarter = 2 * i + u
                    nc.tensor.transpose(
                        bank[:, quarter * BATCH : (quarter + 1) * BATCH],
                        acts_pairs[:, slot * PAIRS_PER_SLOT + u : (slot + 1) * PAIRS_PER_SLOT : 2],
                        identity[:],
                    )
            grouped = stage.tile([P, 2 * BATCH * 4], BF16, align_bytes=64)
            nc.scalar.copy(
                out=grouped[:].bitcast(F32).rearrange("p (i b u) -> p i b u", i=2, u=2),
                in_=bank[:].rearrange("p (i u b) -> p i b u", i=2, u=2),
            )
            columns = slice(two_slots * 2 * BATCH, (two_slots + 1) * 2 * BATCH)
            nc.vector.quantize_mx(
                out=act_codes[:, columns].bitcast(FP8X4), scales=act_scales[:, columns], in_=grouped[:]
            )

        def mx_pass(out, slot, words, columns, start, stop):
            rows = slice(slot * BATCH, (slot + 1) * BATCH)
            if slot == HH_SLOT:
                gate = columns.start // H
                plane = planes[gate * PLANE_ROWS : P, SMALL_BLOCK, columns.start - gate * H : columns.stop - gate * H]
            elif slot == DC_SLOT:
                plane = planes[0:P, SMALL_BLOCK, H + columns.start : H + columns.stop]
            else:
                plane = planes[(slot % PLANES_PER_BLOCK) * PLANE_ROWS : P, slot // PLANES_PER_BLOCK, columns]
            nc.tensor.matmul_mx(
                out=out,
                lhsT=act_codes[:, rows].bitcast(FP8X4),
                lhsT_scale=act_scales[:, rows],
                rhs=words[:, columns].bitcast(FP8X4),
                rhs_scale=plane,
                start=start,
                stop=stop,
            )

        gate_sums = [gates_psum.tile([P, H], F32, name="gate_sum%d" % gate) for gate in EARLY_GATES]
        o_sums = [gates_psum.tile([P, HALF], F32, name="o_sum%d" % half) for half in range(2)]

        def o_passes(slot, words, start, stop):
            for half in range(2):
                mx_pass(o_sums[half][:], slot, words, o_halves[half], start=start, stop=stop)

        for slot in range(IH_SLOTS):
            for gate in EARLY_GATES:
                mx_pass(
                    gate_sums[gate][:],
                    slot,
                    w_ih[:, slot, :],
                    gate_columns(gate),
                    start=(slot == 0),
                    stop=(slot == IH_SLOTS - 1),
                )
            if slot < WHOLE_SLOTS:
                o_passes(slot, w_ih[:, slot, :], start=(slot == 0), stop=False)
            if slot == SMALL_WEIGHTS_AFTER_SLOT:
                for gate in EARLY_GATES:
                    mx_pass(gate_sums[gate][:], HH_SLOT, w_hh[:], gate_columns(gate), start=False, stop=False)
                o_passes(HH_SLOT, w_hh[:], start=False, stop=False)
                bank = work.tile([P, H], F32)
                mx_pass(bank[:], DC_SLOT, w_dc[:], slice(0, H), start=True, stop=True)
                biased = stage.tile([P, H], F32)
                nc.vector.tensor_tensor(out=biased[:], in0=bank[:], in1=bias_all[:, GATES * H : BIAS_COLS], op=ALU.add)
                c_st = keep.tile([P, H], F32)
                nc.scalar.activation(out=c_st[:], in_=biased[:], func=ACT.Tanh)
                cx_adj = keep.tile([P, H], F32)
                nc.vector.scalar_tensor_tensor(
                    out=cx_adj[:],
                    in0=c_st[:],
                    scalar=t_minus_1[:, 0:1],
                    in1=acts[:, DC_SLOT * K_PASS : (DC_SLOT + 1) * K_PASS],
                    op0=ALU.mult,
                    op1=ALU.add,
                )

        def finish_gate(gate, func):
            biased = stage.tile([P, H], F32)
            nc.vector.tensor_tensor(out=biased[:], in0=gate_sums[gate][:], in1=bias_all[:, gate_columns(gate)], op=ALU.add)
            value = keep.tile([P, H], F32, name="gate_value%d" % gate)
            nc.scalar.activation(out=value[:], in_=biased[:], func=func)
            return value

        sigmoid_i = finish_gate(GATE_I, ACT.Sigmoid)
        sigmoid_f = finish_gate(GATE_F, ACT.Sigmoid)
        tanh_g = finish_gate(GATE_G, ACT.Tanh)
        kept = keep.tile([P, H], F32)
        nc.vector.tensor_tensor(out=kept[:], in0=sigmoid_f[:], in1=cx_adj[:], op=ALU.mult)
        fresh = keep.tile([P, H], F32)
        nc.vector.tensor_tensor(out=fresh[:], in0=sigmoid_i[:], in1=tanh_g[:], op=ALU.mult)
        cy = keep.tile([P, H], F32)
        nc.vector.tensor_tensor(out=cy[:], in0=kept[:], in1=fresh[:], op=ALU.add)
        nc.sync.dma_start(out=out_cy, in_=cy[:])
        tanh_cy = keep.tile([P, H], F32)
        nc.scalar.activation(out=tanh_cy[:], in_=cy[:], func=ACT.Tanh)

        for slot in range(WHOLE_SLOTS, IH_SLOTS):
            o_passes(slot, w_ih[:, slot, :], start=False, stop=(slot == IH_SLOTS - 1))
        halves = [slice(half * H // 2, (half + 1) * H // 2) for half in range(2)]
        bias_o = bias_all[:, gate_columns(GATE_O)]
        biased_o = keep.tile([P, H], F32)
        sigmoid_o = keep.tile([P, H], F32)
        hy = keep.tile([P, H], F32)
        for half, columns in enumerate(halves):
            nc.vector.tensor_tensor(out=biased_o[:, columns], in0=o_sums[half][:], in1=bias_o[:, columns], op=ALU.add)
            nc.scalar.activation(out=sigmoid_o[:, columns], in_=biased_o[:, columns], func=ACT.Sigmoid)
        for columns in halves:
            nc.vector.tensor_tensor(out=hy[:, columns], in0=sigmoid_o[:, columns], in1=tanh_cy[:, columns], op=ALU.mult)
            nc.sync.dma_start(out=out_hy[:, columns], in_=hy[:, columns])
